import numpy as np
import ml_dtypes


def mxq(x, axis, fmt="e4m3"):
    dtype, down = {"e4m3": (ml_dtypes.float8_e4m3fn, 7), "e5m2": (ml_dtypes.float8_e5m2, 14)}[fmt]
    v = np.moveaxis(np.asarray(x, np.float32).astype(ml_dtypes.bfloat16).astype(np.float64), axis, -1)
    blocks = v.reshape(v.shape[:-1] + (-1, 32))
    amax = np.abs(blocks).max(-1, keepdims=True)
    byte = np.maximum(np.where(amax > 0, np.frexp(amax)[1] - 1 + 127, 0) - down, 1)
    scale = np.exp2(byte - 127.0)
    codes = (blocks / scale).astype(np.float32).astype(dtype).astype(np.float64)
    return np.moveaxis((codes * scale).reshape(v.shape), -1, axis)


WIDE = False


def mx_kscale(k):
    if not WIDE:
        return np.ones(k)
    levels = np.array([20, -20, 10, -10, 0])
    a = np.random.permutation(np.resize(levels, k // 512 * 4)).reshape(k // 512, 4)
    idx = np.arange(k)
    return np.exp2(a[idx // 512, idx % 128 // 32])


BF16 = ml_dtypes.bfloat16


def bf(x):
    return np.asarray(x, np.float32).astype(BF16)


def f64(x):
    return np.asarray(x).astype(np.float64)


B, T, C, CO, HS, DW, DA, DV, DG = 4, 128, 2048, 2048, 64, 128, 128, 128, 256


def sigmoid(u):
    return 1.0 / (1.0 + np.exp(-u))


def setup_inputs():
    n = np.random.standard_normal
    u = mx_kscale(CO)
    x = bf(n((B, T, C)))
    x_v = bf(n((1, 1, C)) * 0.3)
    W0 = bf(n((CO, C)) / np.sqrt(C))
    v_hid = bf(n((B, T, DV)))
    v2 = bf(n((DV, CO)) / np.sqrt(DV))
    v0 = bf(0.73 + n((1, 1, CO)) * 0.2)
    v_first = bf(n((B, T, CO)))
    g = bf(n((B, T, CO)) * np.exp2(np.random.randint(-12, 1, (B, T, 1))) * 32.0 * u)
    mix = sigmoid(f64(v0) + f64(v_hid) @ f64(v2))
    return {
        "x": x,
        "x_v": x_v,
        "W_v": bf(f64(W0) / u[:, None]),
        "v_hid": v_hid,
        "v2": v2,
        "v0": v0,
        "v_first": v_first,
        "mix": np.asarray(mix, np.float32),
        "grad_out": g,
    }


def reference(x, x_v, W_v, v_hid, v2, v0, v_first, mix, grad_out):
    xvf = f64(x_v)
    dv = f64(grad_out) * (1.0 - f64(mix))
    dxv = mxq(dv, 2, "e5m2") @ mxq(f64(W_v), 0, "e4m3")
    p = dxv * xvf
    nxt = np.concatenate([p[:, 1:], np.zeros_like(p[:, :1])], axis=1)
    return dxv * (1.0 - xvf) + nxt

@@ -1,0 +1,205 @@
+from contextlib import ExitStack
+
+import concourse.mybir as mybir
+from concourse.masks import make_identity
+
+F32 = mybir.dt.float32
+BF16 = mybir.dt.bfloat16
+U32 = mybir.dt.uint32
+U8 = mybir.dt.uint8
+E4M3_X4 = mybir.dt.float8_e4m3fn_x4
+E5M2_X4 = mybir.dt.float8_e5m2_x4
+ALU = mybir.AluOpType
+ACT = mybir.ActivationFunctionType
+
+P = 128
+PACK = 4
+K_PASS = P * PACK
+B, T, C, CO = 4, 128, 2048, 2048
+TOK = B * T
+PASSES = CO // K_PASS
+C_BLOCK = 512
+N_BLOCKS = C // C_BLOCK
+TILES_PER_BLOCK = C_BLOCK // P
+N_TILES = C // P
+N_CHUNKS = N_BLOCKS * PASSES
+HALF = CO // 2
+V_COLS = 320
+LEAD = 7
+RUN = 2
+
+FLOPS = 2 * TOK * CO * C
+BYTES = 2 * CO * C + 2 * TOK * CO + 4 * TOK * CO + 2 * C + 4 * TOK * C
+
+
+def tile_full_tmix_params_pb_v_kernel(tc, x, x_v, W_v, v_hid, v2, v0, v_first, mix, grad_out, out):
+    nc = tc.nc
+    with ExitStack() as stack:
+        keep = stack.enter_context(tc.tile_pool(name="keep", bufs=1))
+        work = stack.enter_context(tc.tile_pool(name="work", bufs=3))
+        psum = stack.enter_context(tc.psum_pool(name="psum", bufs=4))
+        stack.enter_context(tc.manual_schedule())
+
+        xv_rows = keep.tile([P, P], BF16)
+        nc.vector.memset(xv_rows[:], 0.0)
+        nc.scalar.dma_start(out=xv_rows[0:N_TILES, :], in_=x_v.rearrange("a b (r c) -> (a b r) c", c=P))
+        g_in = []
+        mix_in = []
+        for b in range(B):
+            g_in.append(keep.tile([P, CO], BF16, name="g_in%d" % b))
+            nc.sync.dma_start(out=g_in[b][:], in_=grad_out[b])
+            mix_in.append(keep.tile([P, CO], F32, name="mix_in%d" % b))
+            nc.sync.dma_start(out=mix_in[b][:], in_=mix[b])
+        w_raw = []
+        for n in range(N_CHUNKS):
+            block, g = divmod(n, PASSES)
+            rows = W_v[g * K_PASS : (g + 1) * K_PASS, block * C_BLOCK : (block + 1) * C_BLOCK]
+            w_raw.append(keep.tile([P, PACK, C_BLOCK], BF16, name="w_raw%d" % n))
+            nc.sync.dma_start(out=w_raw[n][:], in_=rows.rearrange("(j p) c -> p j c", p=P))
+
+        ident_bf = keep.tile([P, P], BF16)
+        make_identity(nc, ident_bf[:])
+        ident_f32 = keep.tile([P, P], F32)
+        make_identity(nc, ident_f32[:])
+        next_term = []
+        for i in range(3):
+            next_term.append(keep.tile([P, B, T], F32, name="next_term%d" % i))
+            nc.vector.memset(next_term[i][:], 0.0)
+        dv_grouped = keep.tile([P, PASSES, TOK, PACK], BF16, align_bytes=64)
+        for b in range(B):
+            for h in range(CO // HALF):
+                k_cols = slice(h * HALF, (h + 1) * HALF)
+                dv = work.tile([P, HALF], BF16, tag="dv")
+                nc.vector.scalar_tensor_tensor(
+                    out=dv[:],
+                    in0=mix_in[b][:, k_cols],
+                    scalar=1.0,
+                    in1=g_in[b][:, k_cols],
+                    op0=ALU.subtract,
+                    op1=ALU.mult,
+                )
+                dv_t = psum.tile([P, HALF // K_PASS, PACK, T], BF16, tag="tr")
+                for i in range(HALF // P):
+                    nc.tensor.transpose(dv_t[:, i // PACK, i % PACK, :], dv[:, i * P : (i + 1) * P], ident_bf[:])
+                first_pass = h * (HALF // K_PASS)
+                nc.scalar.copy(
+                    out=dv_grouped[:, first_pass : first_pass + HALF // K_PASS, b * T : (b + 1) * T, :],
+                    in_=dv_t[:].rearrange("p g j t -> p g t j"),
+                )
+        xv_t = psum.tile([P, P], BF16, tag="tr")
+        nc.tensor.transpose(xv_t[:], xv_rows[:], ident_bf[:])
+        minus_xv = keep.tile([P, N_TILES], F32)
+        nc.vector.tensor_scalar(out=minus_xv[:], in0=xv_t[:, 0:N_TILES], scalar1=-1.0, scalar2=None, op0=ALU.mult)
+        xv_minus_one = keep.tile([P, N_TILES], F32)
+        nc.vector.tensor_scalar(out=xv_minus_one[:], in0=xv_t[:, 0:N_TILES], scalar1=-1.0, scalar2=None, op0=ALU.add)
+
+        dv_codes = keep.tile([P, PASSES, TOK], U32, align_bytes=64)
+        dv_scales = keep.tile([P, PASSES, TOK], U8, align_bytes=64)
+
+        def quantise_dv(g):
+            nc.vector.quantize_mx(
+                out=dv_codes[:, g, :].bitcast(E5M2_X4),
+                scales=dv_scales[:, g, :],
+                in_=dv_grouped[:, g, :, :].rearrange("p t j -> p (t j)"),
+            )
+
+        w_grouped = {}
+        w_codes = {}
+        w_scales = {}
+
+        def regroup_w(n):
+            w_grouped[n] = work.tile([P, C_BLOCK, PACK], BF16, tag="w_grouped", name="w_grouped%d" % n, align_bytes=64)
+            nc.vector.tensor_copy(
+                out=w_grouped[n][:, 0:V_COLS, :].rearrange("p (c i) j -> p c j i", i=4),
+                in_=w_raw[n][:, :, 0:V_COLS].rearrange("p j (c i) -> p c j i", i=4),
+            )
+            nc.scalar.copy(
+                out=w_grouped[n][:, V_COLS:C_BLOCK, :].rearrange("p (c i) j -> p c j i", i=4),
+                in_=w_raw[n][:, :, V_COLS:C_BLOCK].rearrange("p j (c i) -> p c j i", i=4),
+            )
+
+        def quantise_w(n):
+            block, g = divmod(n, PASSES)
+            if g == 0:
+                w_codes[block] = work.tile([P, PASSES, C_BLOCK], U32, tag="w_codes", name="w_codes%d" % block, align_bytes=64)
+                w_scales[block] = work.tile([P, PASSES, C_BLOCK], U8, tag="w_scales", name="w_scales%d" % block, align_bytes=64)
+            nc.vector.quantize_mx(
+                out=w_codes[block][:, g, :].bitcast(E4M3_X4),
+                scales=w_scales[block][:, g, :],
+                in_=w_grouped[n][:].rearrange("p c j -> p (c j)"),
+            )
+
+        dxv_t = {}
+        blended = {}
+        back = {}
+        out_rows = {}
+
+        def multiply(s):
+            block, i = divmod(s, TILES_PER_BLOCK)
+            c_cols = slice(i * P, (i + 1) * P)
+            dxv_t[s] = psum.tile([P, TOK], F32, tag="dxv_t", name="dxv_t%d" % s)
+            for g in range(PASSES):
+                nc.tensor.matmul_mx(
+                    out=dxv_t[s][:],
+                    lhsT=w_codes[block][:, g, c_cols].bitcast(E4M3_X4),
+                    lhsT_scale=w_scales[block][:, g, c_cols],
+                    rhs=dv_codes[:, g, :].bitcast(E5M2_X4),
+                    rhs_scale=dv_scales[:, g, :],
+                    start=(g == 0),
+                    stop=(g == PASSES - 1),
+                )
+
+        def blend(s):
+            nxt = next_term[s % len(next_term)]
+            nc.scalar.activation(
+                out=nxt[:, :, 0 : T - 1],
+                in_=dxv_t[s][:].rearrange("p (b t) -> p b t", b=B)[:, :, 1:T],
+                func=ACT.Copy,
+                scale=minus_xv[:, s : s + 1],
+            )
+            blended[s] = work.tile([P, TOK], F32, tag="blended", name="blended%d" % s, bufs=2 * RUN + 1)
+            nc.vector.scalar_tensor_tensor(
+                out=blended[s][:],
+                in0=dxv_t[s][:],
+                scalar=xv_minus_one[:, s : s + 1],
+                in1=nxt[:].rearrange("p b t -> p (b t)"),
+                op0=ALU.mult,
+                op1=ALU.add,
+            )
+
+        def transpose_back(s):
+            back[s] = psum.tile([P, B, P], F32, tag="tr", name="back%d" % s)
+            for b in range(B):
+                nc.tensor.transpose(back[s][:, b, :], blended[s][:, b * T : (b + 1) * T], ident_f32[:])
+
+        def store(s):
+            block, i = divmod(s, TILES_PER_BLOCK)
+            if i == 0:
+                out_rows[block] = work.tile([P, B, C_BLOCK], F32, tag="out_rows", name="out_rows%d" % block, bufs=2)
+            nc.scalar.copy(out=out_rows[block][:, :, i * P : (i + 1) * P], in_=back[s][:])
+            if i == TILES_PER_BLOCK - 1:
+                nc.sync.dma_start(
+                    out=out.rearrange("b t c -> t b c")[:, :, block * C_BLOCK : (block + 1) * C_BLOCK],
+                    in_=out_rows[block][:],
+                )
+
+        first_round = -RUN * ((LEAD + RUN - 1) // RUN)
+        for start in range(first_round, N_TILES + RUN, RUN):
+            rounds = range(start, start + RUN)
+            for s in rounds:
+                if 0 <= s < N_TILES:
+                    multiply(s)
+            for s in rounds:
+                if 0 <= s - RUN < N_TILES:
+                    transpose_back(s - RUN)
+            for s in rounds:
+                if 0 <= s < N_TILES:
+                    blend(s)
+                if 0 <= s - RUN < N_TILES:
+                    store(s - RUN)
+                if 0 <= s + LEAD < N_CHUNKS:
+                    regroup_w(s + LEAD)
+                if 0 <= s + LEAD - 1 < N_CHUNKS:
+                    quantise_w(s + LEAD - 1)
+                if 0 <= s + LEAD - 1 < PASSES:
+                    quantise_dv(s + LEAD - 1)

@@ -38,7 +38,6 @@ def tile_full_tmix_params_pb_v_kernel(tc, x, x_v, W_v, v_hid, v2, v0, v_first, m
         keep = stack.enter_context(tc.tile_pool(name="keep", bufs=1))
         work = stack.enter_context(tc.tile_pool(name="work", bufs=3))
         psum = stack.enter_context(tc.psum_pool(name="psum", bufs=4))
-        stack.enter_context(tc.manual_schedule())
 
         xv_rows = keep.tile([P, P], BF16)
         nc.vector.memset(xv_rows[:], 0.0)

@@ -24,8 +24,9 @@ TILES_PER_BLOCK = C_BLOCK // P
 N_TILES = C // P
 N_CHUNKS = N_BLOCKS * PASSES
 HALF = CO // 2
-V_COLS = 320
+V_COLS = 288
 LEAD = 7
+STORE_TILES = 2
 RUN = 2
 
 FLOPS = 2 * TOK * CO * C
@@ -65,6 +66,8 @@ def tile_full_tmix_params_pb_v_kernel(tc, x, x_v, W_v, v_hid, v2, v0, v_first, m
             next_term.append(keep.tile([P, B, T], F32, name="next_term%d" % i))
             nc.vector.memset(next_term[i][:], 0.0)
         dv_grouped = keep.tile([P, PASSES, TOK, PACK], BF16, align_bytes=64)
+        dv_codes = keep.tile([P, PASSES, TOK], U32, align_bytes=64)
+        dv_scales = keep.tile([P, PASSES, TOK], U8, align_bytes=64)
         for b in range(B):
             for h in range(CO // HALF):
                 k_cols = slice(h * HALF, (h + 1) * HALF)
@@ -85,22 +88,18 @@ def tile_full_tmix_params_pb_v_kernel(tc, x, x_v, W_v, v_hid, v2, v0, v_first, m
                     out=dv_grouped[:, first_pass : first_pass + HALF // K_PASS, b * T : (b + 1) * T, :],
                     in_=dv_t[:].rearrange("p g j t -> p g t j"),
                 )
+                for g in range(first_pass, first_pass + HALF // K_PASS):
+                    nc.vector.quantize_mx(
+                        out=dv_codes[:, g, b * T : (b + 1) * T].bitcast(E5M2_X4),
+                        scales=dv_scales[:, g, b * T : (b + 1) * T],
+                        in_=dv_grouped[:, g, b * T : (b + 1) * T, :].rearrange("p t j -> p (t j)"),
+                    )
         xv_t = psum.tile([P, P], BF16, tag="tr")
         nc.tensor.transpose(xv_t[:], xv_rows[:], ident_bf[:])
         minus_xv = keep.tile([P, N_TILES], F32)
         nc.vector.tensor_scalar(out=minus_xv[:], in0=xv_t[:, 0:N_TILES], scalar1=-1.0, scalar2=None, op0=ALU.mult)
         xv_minus_one = keep.tile([P, N_TILES], F32)
         nc.vector.tensor_scalar(out=xv_minus_one[:], in0=xv_t[:, 0:N_TILES], scalar1=-1.0, scalar2=None, op0=ALU.add)
-
-        dv_codes = keep.tile([P, PASSES, TOK], U32, align_bytes=64)
-        dv_scales = keep.tile([P, PASSES, TOK], U8, align_bytes=64)
-
-        def quantise_dv(g):
-            nc.vector.quantize_mx(
-                out=dv_codes[:, g, :].bitcast(E5M2_X4),
-                scales=dv_scales[:, g, :],
-                in_=dv_grouped[:, g, :, :].rearrange("p t j -> p (t j)"),
-            )
 
         w_grouped = {}
         w_codes = {}
@@ -172,15 +171,13 @@ def tile_full_tmix_params_pb_v_kernel(tc, x, x_v, W_v, v_hid, v2, v0, v_first, m
                 nc.tensor.transpose(back[s][:, b, :], blended[s][:, b * T : (b + 1) * T], ident_f32[:])
 
         def store(s):
-            block, i = divmod(s, TILES_PER_BLOCK)
+            piece, i = divmod(s, STORE_TILES)
             if i == 0:
-                out_rows[block] = work.tile([P, B, C_BLOCK], F32, tag="out_rows", name="out_rows%d" % block, bufs=2)
-            nc.scalar.copy(out=out_rows[block][:, :, i * P : (i + 1) * P], in_=back[s][:])
-            if i == TILES_PER_BLOCK - 1:
-                nc.sync.dma_start(
-                    out=out.rearrange("b t c -> t b c")[:, :, block * C_BLOCK : (block + 1) * C_BLOCK],
-                    in_=out_rows[block][:],
-                )
+                out_rows[piece] = work.tile([P, B, STORE_TILES * P], F32, tag="out_rows", name="out_rows%d" % piece)
+            nc.scalar.copy(out=out_rows[piece][:, :, i * P : (i + 1) * P], in_=back[s][:])
+            if i == STORE_TILES - 1:
+                c_cols = slice(piece * STORE_TILES * P, (piece + 1) * STORE_TILES * P)
+                nc.sync.dma_start(out=out.rearrange("b t c -> t b c")[:, :, c_cols], in_=out_rows[piece][:])
 
         first_round = -RUN * ((LEAD + RUN - 1) // RUN)
         for start in range(first_round, N_TILES + RUN, RUN):
@@ -200,5 +197,3 @@ def tile_full_tmix_params_pb_v_kernel(tc, x, x_v, W_v, v_hid, v2, v0, v_first, m
                     regroup_w(s + LEAD)
                 if 0 <= s + LEAD - 1 < N_CHUNKS:
                     quantise_w(s + LEAD - 1)
-                if 0 <= s + LEAD - 1 < PASSES:
-                    quantise_dv(s + LEAD - 1)

@@ -15,6 +15,7 @@ ACT = mybir.ActivationFunctionType
 P = 128
 PACK = 4
 K_PASS = P * PACK
+WORDS = 2
 B, T, C, CO = 4, 128, 2048, 2048
 TOK = B * T
 PASSES = CO // K_PASS
@@ -24,10 +25,12 @@ TILES_PER_BLOCK = C_BLOCK // P
 N_TILES = C // P
 N_CHUNKS = N_BLOCKS * PASSES
 HALF = CO // 2
-V_COLS = 288
-LEAD = 7
+HALF_PASSES = HALF // K_PASS
+V_COLS = 320
+V_COLS_FIRST_BLOCK = 240
 STORE_TILES = 2
-RUN = 2
+ACC_BANKS = 6
+TR_BANKS = 2
 
 FLOPS = 2 * TOK * CO * C
 BYTES = 2 * CO * C + 2 * TOK * CO + 4 * TOK * CO + 2 * C + 4 * TOK * C
@@ -38,62 +41,63 @@ def tile_full_tmix_params_pb_v_kernel(tc, x, x_v, W_v, v_hid, v2, v0, v_first, m
     with ExitStack() as stack:
         keep = stack.enter_context(tc.tile_pool(name="keep", bufs=1))
         work = stack.enter_context(tc.tile_pool(name="work", bufs=3))
-        psum = stack.enter_context(tc.psum_pool(name="psum", bufs=4))
+        psum = stack.enter_context(tc.psum_pool(name="psum", bufs=TR_BANKS))
 
         xv_rows = keep.tile([P, P], BF16)
         nc.vector.memset(xv_rows[:], 0.0)
         nc.scalar.dma_start(out=xv_rows[0:N_TILES, :], in_=x_v.rearrange("a b (r c) -> (a b r) c", c=P))
-        g_in = []
-        mix_in = []
-        for b in range(B):
-            g_in.append(keep.tile([P, CO], BF16, name="g_in%d" % b))
-            nc.sync.dma_start(out=g_in[b][:], in_=grad_out[b])
-            mix_in.append(keep.tile([P, CO], F32, name="mix_in%d" % b))
-            nc.sync.dma_start(out=mix_in[b][:], in_=mix[b])
+        units = [(b, h) for b in range(B) for h in range(CO // HALF)]
+        g_in = {}
+        mix_in = {}
+        for b, h in units:
+            k_cols = slice(h * HALF, (h + 1) * HALF)
+            g_in[b, h] = keep.tile([P, HALF], BF16, name="g_in%d_%d" % (b, h))
+            nc.sync.dma_start(out=g_in[b, h][:], in_=grad_out[b][:, k_cols])
+            mix_in[b, h] = keep.tile([P, HALF], F32, name="mix_in%d_%d" % (b, h))
+            nc.sync.dma_start(out=mix_in[b, h][:], in_=mix[b][:, k_cols])
         w_raw = []
         for n in range(N_CHUNKS):
             block, g = divmod(n, PASSES)
             rows = W_v[g * K_PASS : (g + 1) * K_PASS, block * C_BLOCK : (block + 1) * C_BLOCK]
             w_raw.append(keep.tile([P, PACK, C_BLOCK], BF16, name="w_raw%d" % n))
-            nc.sync.dma_start(out=w_raw[n][:], in_=rows.rearrange("(j p) c -> p j c", p=P))
+            nc.sync.dma_start(out=w_raw[n][:], in_=rows.rearrange("(p j) c -> p j c", j=PACK))
 
         ident_bf = keep.tile([P, P], BF16)
         make_identity(nc, ident_bf[:])
         ident_f32 = keep.tile([P, P], F32)
         make_identity(nc, ident_f32[:])
         next_term = []
-        for i in range(3):
+        for i in range(TILES_PER_BLOCK):
             next_term.append(keep.tile([P, B, T], F32, name="next_term%d" % i))
             nc.vector.memset(next_term[i][:], 0.0)
+
         dv_grouped = keep.tile([P, PASSES, TOK, PACK], BF16, align_bytes=64)
         dv_codes = keep.tile([P, PASSES, TOK], U32, align_bytes=64)
         dv_scales = keep.tile([P, PASSES, TOK], U8, align_bytes=64)
-        for b in range(B):
-            for h in range(CO // HALF):
-                k_cols = slice(h * HALF, (h + 1) * HALF)
-                dv = work.tile([P, HALF], BF16, tag="dv")
-                nc.vector.scalar_tensor_tensor(
-                    out=dv[:],
-                    in0=mix_in[b][:, k_cols],
-                    scalar=1.0,
-                    in1=g_in[b][:, k_cols],
-                    op0=ALU.subtract,
-                    op1=ALU.mult,
-                )
-                dv_t = psum.tile([P, HALF // K_PASS, PACK, T], BF16, tag="tr")
-                for i in range(HALF // P):
-                    nc.tensor.transpose(dv_t[:, i // PACK, i % PACK, :], dv[:, i * P : (i + 1) * P], ident_bf[:])
-                first_pass = h * (HALF // K_PASS)
-                nc.scalar.copy(
-                    out=dv_grouped[:, first_pass : first_pass + HALF // K_PASS, b * T : (b + 1) * T, :],
-                    in_=dv_t[:].rearrange("p g j t -> p g t j"),
-                )
-                for g in range(first_pass, first_pass + HALF // K_PASS):
-                    nc.vector.quantize_mx(
-                        out=dv_codes[:, g, b * T : (b + 1) * T].bitcast(E5M2_X4),
-                        scales=dv_scales[:, g, b * T : (b + 1) * T],
-                        in_=dv_grouped[:, g, b * T : (b + 1) * T, :].rearrange("p t j -> p (t j)"),
+        for b, h in units:
+            dv = work.tile([P, HALF], BF16, tag="dv")
+            nc.vector.scalar_tensor_tensor(
+                out=dv[:], in0=mix_in[b, h][:], scalar=1.0, in1=g_in[b, h][:], op0=ALU.subtract, op1=ALU.mult
+            )
+            words = dv[:].bitcast(F32)
+            dv_t = psum.tile([P, HALF_PASSES, WORDS, T], F32, tag="tr")
+            for i in range(HALF_PASSES):
+                for u in range(WORDS):
+                    nc.tensor.transpose(
+                        dv_t[:, i, u, :], words[:, i * WORDS * P + u : (i + 1) * WORDS * P : WORDS], ident_f32[:]
                     )
+            first_pass = h * HALF_PASSES
+            tokens = slice(b * T, (b + 1) * T)
+            nc.scalar.copy(
+                out=dv_grouped[:, first_pass : first_pass + HALF_PASSES, tokens, :].bitcast(F32),
+                in_=dv_t[:].rearrange("p g u t -> p g t u"),
+            )
+            for g in range(first_pass, first_pass + HALF_PASSES):
+                nc.vector.quantize_mx(
+                    out=dv_codes[:, g, tokens].bitcast(E5M2_X4),
+                    scales=dv_scales[:, g, tokens],
+                    in_=dv_grouped[:, g, tokens, :].rearrange("p t j -> p (t j)"),
+                )
         xv_t = psum.tile([P, P], BF16, tag="tr")
         nc.tensor.transpose(xv_t[:], xv_rows[:], ident_bf[:])
         minus_xv = keep.tile([P, N_TILES], F32)
@@ -104,48 +108,49 @@ def tile_full_tmix_params_pb_v_kernel(tc, x, x_v, W_v, v_hid, v2, v0, v_first, m
         w_grouped = {}
         w_codes = {}
         w_scales = {}
+        dxv_t = {}
 
         def regroup_w(n):
             w_grouped[n] = work.tile([P, C_BLOCK, PACK], BF16, tag="w_grouped", name="w_grouped%d" % n, align_bytes=64)
+            v_cols = V_COLS_FIRST_BLOCK if n < PASSES else V_COLS
             nc.vector.tensor_copy(
-                out=w_grouped[n][:, 0:V_COLS, :].rearrange("p (c i) j -> p c j i", i=4),
-                in_=w_raw[n][:, :, 0:V_COLS].rearrange("p j (c i) -> p c j i", i=4),
+                out=w_grouped[n][:, 0:v_cols, :].rearrange("p (c i) j -> p c j i", i=4),
+                in_=w_raw[n][:, :, 0:v_cols].rearrange("p j (c i) -> p c j i", i=4),
             )
             nc.scalar.copy(
-                out=w_grouped[n][:, V_COLS:C_BLOCK, :].rearrange("p (c i) j -> p c j i", i=4),
-                in_=w_raw[n][:, :, V_COLS:C_BLOCK].rearrange("p j (c i) -> p c j i", i=4),
+                out=w_grouped[n][:, v_cols:C_BLOCK, :].rearrange("p (c i) j -> p c j i", i=4),
+                in_=w_raw[n][:, :, v_cols:C_BLOCK].rearrange("p j (c i) -> p c j i", i=4),
             )
 
         def quantise_w(n):
-            block, g = divmod(n, PASSES)
-            if g == 0:
-                w_codes[block] = work.tile([P, PASSES, C_BLOCK], U32, tag="w_codes", name="w_codes%d" % block, align_bytes=64)
-                w_scales[block] = work.tile([P, PASSES, C_BLOCK], U8, tag="w_scales", name="w_scales%d" % block, align_bytes=64)
+            w_codes[n] = work.tile([P, C_BLOCK], U32, tag="w_codes", name="w_codes%d" % n, align_bytes=64, bufs=6)
+            w_scales[n] = work.tile([P, C_BLOCK], U8, tag="w_scales", name="w_scales%d" % n, align_bytes=64, bufs=6)
             nc.vector.quantize_mx(
-                out=w_codes[block][:, g, :].bitcast(E4M3_X4),
-                scales=w_scales[block][:, g, :],
+                out=w_codes[n][:].bitcast(E4M3_X4),
+                scales=w_scales[n][:],
                 in_=w_grouped[n][:].rearrange("p c j -> p (c j)"),
             )
 
-        dxv_t = {}
-        blended = {}
-        back = {}
-        out_rows = {}
-
-        def multiply(s):
-            block, i = divmod(s, TILES_PER_BLOCK)
-            c_cols = slice(i * P, (i + 1) * P)
-            dxv_t[s] = psum.tile([P, TOK], F32, tag="dxv_t", name="dxv_t%d" % s)
-            for g in range(PASSES):
+        def multiply(n):
+            block, g = divmod(n, PASSES)
+            for i in range(TILES_PER_BLOCK):
+                s = block * TILES_PER_BLOCK + i
+                if g == 0:
+                    dxv_t[s] = psum.tile([P, TOK], F32, tag="dxv_t", name="dxv_t%d" % s, bufs=ACC_BANKS)
+                c_cols = slice(i * P, (i + 1) * P)
                 nc.tensor.matmul_mx(
                     out=dxv_t[s][:],
-                    lhsT=w_codes[block][:, g, c_cols].bitcast(E4M3_X4),
-                    lhsT_scale=w_scales[block][:, g, c_cols],
+                    lhsT=w_codes[n][:, c_cols].bitcast(E4M3_X4),
+                    lhsT_scale=w_scales[n][:, c_cols],
                     rhs=dv_codes[:, g, :].bitcast(E5M2_X4),
                     rhs_scale=dv_scales[:, g, :],
                     start=(g == 0),
                     stop=(g == PASSES - 1),
                 )
+
+        blended = {}
+        back = {}
+        out_rows = {}
 
         def blend(s):
             nxt = next_term[s % len(next_term)]
@@ -155,7 +160,7 @@ def tile_full_tmix_params_pb_v_kernel(tc, x, x_v, W_v, v_hid, v2, v0, v_first, m
                 func=ACT.Copy,
                 scale=minus_xv[:, s : s + 1],
             )
-            blended[s] = work.tile([P, TOK], F32, tag="blended", name="blended%d" % s, bufs=2 * RUN + 1)
+            blended[s] = work.tile([P, TOK], F32, tag="blended", name="blended%d" % s, bufs=6)
             nc.vector.scalar_tensor_tensor(
                 out=blended[s][:],
                 in0=dxv_t[s][:],
@@ -174,26 +179,26 @@ def tile_full_tmix_params_pb_v_kernel(tc, x, x_v, W_v, v_hid, v2, v0, v_first, m
             piece, i = divmod(s, STORE_TILES)
             if i == 0:
                 out_rows[piece] = work.tile([P, B, STORE_TILES * P], F32, tag="out_rows", name="out_rows%d" % piece)
-            nc.scalar.copy(out=out_rows[piece][:, :, i * P : (i + 1) * P], in_=back[s][:])
+            if i == 0 or s < N_TILES - TILES_PER_BLOCK:
+                nc.scalar.copy(out=out_rows[piece][:, :, i * P : (i + 1) * P], in_=back[s][:])
+            else:
+                nc.vector.tensor_copy(out=out_rows[piece][:, :, i * P : (i + 1) * P], in_=back[s][:])
             if i == STORE_TILES - 1:
                 c_cols = slice(piece * STORE_TILES * P, (piece + 1) * STORE_TILES * P)
                 nc.sync.dma_start(out=out.rearrange("b t c -> t b c")[:, :, c_cols], in_=out_rows[piece][:])
 
-        first_round = -RUN * ((LEAD + RUN - 1) // RUN)
-        for start in range(first_round, N_TILES + RUN, RUN):
-            rounds = range(start, start + RUN)
-            for s in rounds:
-                if 0 <= s < N_TILES:
-                    multiply(s)
-            for s in rounds:
-                if 0 <= s - RUN < N_TILES:
-                    transpose_back(s - RUN)
-            for s in rounds:
-                if 0 <= s < N_TILES:
-                    blend(s)
-                if 0 <= s - RUN < N_TILES:
-                    store(s - RUN)
-                if 0 <= s + LEAD < N_CHUNKS:
-                    regroup_w(s + LEAD)
-                if 0 <= s + LEAD - 1 < N_CHUNKS:
-                    quantise_w(s + LEAD - 1)
+        for r in range(N_CHUNKS + 2 + TILES_PER_BLOCK + 2):
+            if 0 <= r - 2 < N_CHUNKS:
+                multiply(r - 2)
+            done_block, step = divmod(r - 2 - (PASSES - 1), PASSES)
+            if 0 <= done_block < N_BLOCKS and step < 2:
+                blend(done_block * TILES_PER_BLOCK + 2 * step)
+                blend(done_block * TILES_PER_BLOCK + 2 * step + 1)
+            if 0 <= r - 6 < N_TILES:
+                transpose_back(r - 6)
+            if 0 <= r - 7 < N_TILES:
+                store(r - 7)
+            if 0 <= r - 1 < N_CHUNKS:
+                quantise_w(r - 1)
+            if 0 <= r < N_CHUNKS:
+                regroup_w(r)

@@ -28,6 +28,7 @@ HALF = CO // 2
 HALF_PASSES = HALF // K_PASS
 V_COLS = 320
 V_COLS_FIRST_BLOCK = 240
+RUN = 8
 STORE_TILES = 2
 ACC_BANKS = 6
 TR_BANKS = 2
@@ -114,12 +115,12 @@ def tile_full_tmix_params_pb_v_kernel(tc, x, x_v, W_v, v_hid, v2, v0, v_first, m
             w_grouped[n] = work.tile([P, C_BLOCK, PACK], BF16, tag="w_grouped", name="w_grouped%d" % n, align_bytes=64)
             v_cols = V_COLS_FIRST_BLOCK if n < PASSES else V_COLS
             nc.vector.tensor_copy(
-                out=w_grouped[n][:, 0:v_cols, :].rearrange("p (c i) j -> p c j i", i=4),
-                in_=w_raw[n][:, :, 0:v_cols].rearrange("p j (c i) -> p c j i", i=4),
+                out=w_grouped[n][:, 0:v_cols, :].rearrange("p (c i) j -> p c j i", i=RUN),
+                in_=w_raw[n][:, :, 0:v_cols].rearrange("p j (c i) -> p c j i", i=RUN),
             )
             nc.scalar.copy(
-                out=w_grouped[n][:, v_cols:C_BLOCK, :].rearrange("p (c i) j -> p c j i", i=4),
-                in_=w_raw[n][:, :, v_cols:C_BLOCK].rearrange("p j (c i) -> p c j i", i=4),
+                out=w_grouped[n][:, v_cols:C_BLOCK, :].rearrange("p (c i) j -> p c j i", i=RUN),
+                in_=w_raw[n][:, :, v_cols:C_BLOCK].rearrange("p j (c i) -> p c j i", i=RUN),
             )
 
         def quantise_w(n):

@@ -155,12 +155,13 @@ def tile_full_tmix_params_pb_v_kernel(tc, x, x_v, W_v, v_hid, v2, v0, v_first, m
 
         def blend(s):
             nxt = next_term[s % len(next_term)]
-            nc.scalar.activation(
-                out=nxt[:, :, 0 : T - 1],
-                in_=dxv_t[s][:].rearrange("p (b t) -> p b t", b=B)[:, :, 1:T],
-                func=ACT.Copy,
-                scale=minus_xv[:, s : s + 1],
-            )
+            later_tokens = dxv_t[s][:].rearrange("p (b t) -> p b t", b=B)[:, :, 1:T]
+            if s % 2 == 0 or s < N_TILES - TILES_PER_BLOCK:
+                nc.scalar.activation(out=nxt[:, :, 0 : T - 1], in_=later_tokens, func=ACT.Copy, scale=minus_xv[:, s : s + 1])
+            else:
+                nc.vector.tensor_scalar(
+                    out=nxt[:, :, 0 : T - 1], in0=later_tokens, scalar1=minus_xv[:, s : s + 1], scalar2=None, op0=ALU.mult
+                )
             blended[s] = work.tile([P, TOK], F32, tag="blended", name="blended%d" % s, bufs=6)
             nc.vector.scalar_tensor_tensor(
                 out=blended[s][:],
@@ -184,13 +185,18 @@ def tile_full_tmix_params_pb_v_kernel(tc, x, x_v, W_v, v_hid, v2, v0, v_first, m
                 nc.scalar.copy(out=out_rows[piece][:, :, i * P : (i + 1) * P], in_=back[s][:])
             else:
                 nc.vector.tensor_copy(out=out_rows[piece][:, :, i * P : (i + 1) * P], in_=back[s][:])
-            if i == STORE_TILES - 1:
+            if s >= N_TILES - TILES_PER_BLOCK:
+                nc.sync.dma_start(
+                    out=out.rearrange("b t c -> t b c")[:, :, s * P : (s + 1) * P], in_=out_rows[piece][:, :, i * P : (i + 1) * P]
+                )
+            elif i == STORE_TILES - 1:
                 c_cols = slice(piece * STORE_TILES * P, (piece + 1) * STORE_TILES * P)
                 nc.sync.dma_start(out=out.rearrange("b t c -> t b c")[:, :, c_cols], in_=out_rows[piece][:])
 
         for r in range(N_CHUNKS + 2 + TILES_PER_BLOCK + 2):
             if 0 <= r - 2 < N_CHUNKS:
-                multiply(r - 2)
+                with tc.high_priority():
+                    multiply(r - 2)
             done_block, step = divmod(r - 2 - (PASSES - 1), PASSES)
             if 0 <= done_block < N_BLOCKS and step < 2:
                 blend(done_block * TILES_PER_BLOCK + 2 * step)

@@ -173,7 +173,10 @@ def tile_full_tmix_params_pb_v_kernel(tc, x, x_v, W_v, v_hid, v2, v0, v_first, m
             )
 
         def transpose_back(s):
-            back[s] = psum.tile([P, B, P], F32, tag="tr", name="back%d" % s)
+            if s < N_TILES - TILES_PER_BLOCK:
+                back[s] = psum.tile([P, B, P], F32, tag="tr", name="back%d" % s)
+            else:
+                back[s] = psum.tile([P, B, P], F32, tag="dxv_t", name="back%d" % s, bufs=ACC_BANKS)
             for b in range(B):
                 nc.tensor.transpose(back[s][:, b, :], blended[s][:, b * T : (b + 1) * T], ident_f32[:])
 
@@ -198,9 +201,13 @@ def tile_full_tmix_params_pb_v_kernel(tc, x, x_v, W_v, v_hid, v2, v0, v_first, m
                 with tc.high_priority():
                     multiply(r - 2)
             done_block, step = divmod(r - 2 - (PASSES - 1), PASSES)
-            if 0 <= done_block < N_BLOCKS and step < 2:
+            if 0 <= done_block < N_BLOCKS - 1 and step < 2:
                 blend(done_block * TILES_PER_BLOCK + 2 * step)
                 blend(done_block * TILES_PER_BLOCK + 2 * step + 1)
+            if done_block == N_BLOCKS - 1 and step < 2:
+                with tc.high_priority():
+                    blend(done_block * TILES_PER_BLOCK + 2 * step)
+                    blend(done_block * TILES_PER_BLOCK + 2 * step + 1)
             if 0 <= r - 6 < N_TILES:
                 transpose_back(r - 6)
             if 0 <= r - 7 < N_TILES:

@@ -112,7 +112,7 @@ def tile_full_tmix_params_pb_v_kernel(tc, x, x_v, W_v, v_hid, v2, v0, v_first, m
         dxv_t = {}
 
         def regroup_w(n):
-            w_grouped[n] = work.tile([P, C_BLOCK, PACK], BF16, tag="w_grouped", name="w_grouped%d" % n, align_bytes=64)
+            w_grouped[n] = work.tile([P, C_BLOCK, PACK], BF16, tag="w_grouped", name="w_grouped%d" % n, align_bytes=64, bufs=4)
             v_cols = V_COLS_FIRST_BLOCK if n < PASSES else V_COLS
             nc.vector.tensor_copy(
                 out=w_grouped[n][:, 0:v_cols, :].rearrange("p (c i) j -> p c j i", i=RUN),
@@ -124,8 +124,8 @@ def tile_full_tmix_params_pb_v_kernel(tc, x, x_v, W_v, v_hid, v2, v0, v_first, m
             )
 
         def quantise_w(n):
-            w_codes[n] = work.tile([P, C_BLOCK], U32, tag="w_codes", name="w_codes%d" % n, align_bytes=64, bufs=6)
-            w_scales[n] = work.tile([P, C_BLOCK], U8, tag="w_scales", name="w_scales%d" % n, align_bytes=64, bufs=6)
+            w_codes[n] = work.tile([P, C_BLOCK], U32, tag="w_codes", name="w_codes%d" % n, align_bytes=64, bufs=8)
+            w_scales[n] = work.tile([P, C_BLOCK], U8, tag="w_scales", name="w_scales%d" % n, align_bytes=64, bufs=8)
             nc.vector.quantize_mx(
                 out=w_codes[n][:].bitcast(E4M3_X4),
                 scales=w_scales[n][:],
@@ -162,7 +162,7 @@ def tile_full_tmix_params_pb_v_kernel(tc, x, x_v, W_v, v_hid, v2, v0, v_first, m
                 nc.vector.tensor_scalar(
                     out=nxt[:, :, 0 : T - 1], in0=later_tokens, scalar1=minus_xv[:, s : s + 1], scalar2=None, op0=ALU.mult
                 )
-            blended[s] = work.tile([P, TOK], F32, tag="blended", name="blended%d" % s, bufs=6)
+            blended[s] = work.tile([P, TOK], F32, tag="blended", name="blended%d" % s, bufs=8)
             nc.vector.scalar_tensor_tensor(
                 out=blended[s][:],
                 in0=dxv_t[s][:],
@@ -183,7 +183,7 @@ def tile_full_tmix_params_pb_v_kernel(tc, x, x_v, W_v, v_hid, v2, v0, v_first, m
         def store(s):
             piece, i = divmod(s, STORE_TILES)
             if i == 0:
-                out_rows[piece] = work.tile([P, B, STORE_TILES * P], F32, tag="out_rows", name="out_rows%d" % piece)
+                out_rows[piece] = work.tile([P, B, STORE_TILES * P], F32, tag="out_rows", name="out_rows%d" % piece, bufs=5)
             if i == 0 or s < N_TILES - TILES_PER_BLOCK:
                 nc.scalar.copy(out=out_rows[piece][:, :, i * P : (i + 1) * P], in_=back[s][:])
             else:

from contextlib import ExitStack

import concourse.mybir as mybir
from concourse.masks import make_identity

F32 = mybir.dt.float32
BF16 = mybir.dt.bfloat16
U32 = mybir.dt.uint32
U8 = mybir.dt.uint8
E4M3_X4 = mybir.dt.float8_e4m3fn_x4
E5M2_X4 = mybir.dt.float8_e5m2_x4
ALU = mybir.AluOpType
ACT = mybir.ActivationFunctionType

P = 128
PACK = 4
K_PASS = P * PACK
WORDS = 2
B, T, C, CO = 4, 128, 2048, 2048
TOK = B * T
PASSES = CO // K_PASS
C_BLOCK = 512
N_BLOCKS = C // C_BLOCK
TILES_PER_BLOCK = C_BLOCK // P
N_TILES = C // P
N_CHUNKS = N_BLOCKS * PASSES
HALF = CO // 2
HALF_PASSES = HALF // K_PASS
V_COLS = 320
V_COLS_FIRST_BLOCK = 240
RUN = 8
STORE_TILES = 2
ACC_BANKS = 6
TR_BANKS = 2

FLOPS = 2 * TOK * CO * C
BYTES = 2 * CO * C + 2 * TOK * CO + 4 * TOK * CO + 2 * C + 4 * TOK * C


def tile_full_tmix_params_pb_v_kernel(tc, x, x_v, W_v, v_hid, v2, v0, v_first, mix, grad_out, out):
    nc = tc.nc
    with ExitStack() as stack:
        keep = stack.enter_context(tc.tile_pool(name="keep", bufs=1))
        work = stack.enter_context(tc.tile_pool(name="work", bufs=3))
        psum = stack.enter_context(tc.psum_pool(name="psum", bufs=TR_BANKS))

        xv_rows = keep.tile([P, P], BF16)
        nc.vector.memset(xv_rows[:], 0.0)
        nc.scalar.dma_start(out=xv_rows[0:N_TILES, :], in_=x_v.rearrange("a b (r c) -> (a b r) c", c=P))
        units = [(b, h) for b in range(B) for h in range(CO // HALF)]
        g_in = {}
        mix_in = {}
        for b, h in units:
            k_cols = slice(h * HALF, (h + 1) * HALF)
            g_in[b, h] = keep.tile([P, HALF], BF16, name="g_in%d_%d" % (b, h))
            nc.sync.dma_start(out=g_in[b, h][:], in_=grad_out[b][:, k_cols])
            mix_in[b, h] = keep.tile([P, HALF], F32, name="mix_in%d_%d" % (b, h))
            nc.sync.dma_start(out=mix_in[b, h][:], in_=mix[b][:, k_cols])
        w_raw = []
        for n in range(N_CHUNKS):
            block, g = divmod(n, PASSES)
            rows = W_v[g * K_PASS : (g + 1) * K_PASS, block * C_BLOCK : (block + 1) * C_BLOCK]
            w_raw.append(keep.tile([P, PACK, C_BLOCK], BF16, name="w_raw%d" % n))
            nc.sync.dma_start(out=w_raw[n][:], in_=rows.rearrange("(p j) c -> p j c", j=PACK))

        ident_bf = keep.tile([P, P], BF16)
        make_identity(nc, ident_bf[:])
        ident_f32 = keep.tile([P, P], F32)
        make_identity(nc, ident_f32[:])
        next_term = []
        for i in range(TILES_PER_BLOCK):
            next_term.append(keep.tile([P, B, T], F32, name="next_term%d" % i))
            nc.vector.memset(next_term[i][:], 0.0)

        dv_grouped = keep.tile([P, PASSES, TOK, PACK], BF16, align_bytes=64)
        dv_codes = keep.tile([P, PASSES, TOK], U32, align_bytes=64)
        dv_scales = keep.tile([P, PASSES, TOK], U8, align_bytes=64)
        for b, h in units:
            dv = work.tile([P, HALF], BF16, tag="dv")
            nc.vector.scalar_tensor_tensor(
                out=dv[:], in0=mix_in[b, h][:], scalar=1.0, in1=g_in[b, h][:], op0=ALU.subtract, op1=ALU.mult
            )
            words = dv[:].bitcast(F32)
            dv_t = psum.tile([P, HALF_PASSES, WORDS, T], F32, tag="tr")
            for i in range(HALF_PASSES):
                for u in range(WORDS):
                    nc.tensor.transpose(
                        dv_t[:, i, u, :], words[:, i * WORDS * P + u : (i + 1) * WORDS * P : WORDS], ident_f32[:]
                    )
            first_pass = h * HALF_PASSES
            tokens = slice(b * T, (b + 1) * T)
            nc.scalar.copy(
                out=dv_grouped[:, first_pass : first_pass + HALF_PASSES, tokens, :].bitcast(F32),
                in_=dv_t[:].rearrange("p g u t -> p g t u"),
            )
            for g in range(first_pass, first_pass + HALF_PASSES):
                nc.vector.quantize_mx(
                    out=dv_codes[:, g, tokens].bitcast(E5M2_X4),
                    scales=dv_scales[:, g, tokens],
                    in_=dv_grouped[:, g, tokens, :].rearrange("p t j -> p (t j)"),
                )
        xv_t = psum.tile([P, P], BF16, tag="tr")
        nc.tensor.transpose(xv_t[:], xv_rows[:], ident_bf[:])
        minus_xv = keep.tile([P, N_TILES], F32)
        nc.vector.tensor_scalar(out=minus_xv[:], in0=xv_t[:, 0:N_TILES], scalar1=-1.0, scalar2=None, op0=ALU.mult)
        xv_minus_one = keep.tile([P, N_TILES], F32)
        nc.vector.tensor_scalar(out=xv_minus_one[:], in0=xv_t[:, 0:N_TILES], scalar1=-1.0, scalar2=None, op0=ALU.add)

        w_grouped = {}
        w_codes = {}
        w_scales = {}
        dxv_t = {}

        def regroup_w(n):
            w_grouped[n] = work.tile([P, C_BLOCK, PACK], BF16, tag="w_grouped", name="w_grouped%d" % n, align_bytes=64, bufs=4)
            v_cols = V_COLS_FIRST_BLOCK if n < PASSES else V_COLS
            nc.vector.tensor_copy(
                out=w_grouped[n][:, 0:v_cols, :].rearrange("p (c i) j -> p c j i", i=RUN),
                in_=w_raw[n][:, :, 0:v_cols].rearrange("p j (c i) -> p c j i", i=RUN),
            )
            nc.scalar.copy(
                out=w_grouped[n][:, v_cols:C_BLOCK, :].rearrange("p (c i) j -> p c j i", i=RUN),
                in_=w_raw[n][:, :, v_cols:C_BLOCK].rearrange("p j (c i) -> p c j i", i=RUN),
            )

        def quantise_w(n):
            w_codes[n] = work.tile([P, C_BLOCK], U32, tag="w_codes", name="w_codes%d" % n, align_bytes=64, bufs=8)
            w_scales[n] = work.tile([P, C_BLOCK], U8, tag="w_scales", name="w_scales%d" % n, align_bytes=64, bufs=8)
            nc.vector.quantize_mx(
                out=w_codes[n][:].bitcast(E4M3_X4),
                scales=w_scales[n][:],
                in_=w_grouped[n][:].rearrange("p c j -> p (c j)"),
            )

        def multiply(n):
            block, g = divmod(n, PASSES)
            for i in range(TILES_PER_BLOCK):
                s = block * TILES_PER_BLOCK + i
                if g == 0:
                    dxv_t[s] = psum.tile([P, TOK], F32, tag="dxv_t", name="dxv_t%d" % s, bufs=ACC_BANKS)
                c_cols = slice(i * P, (i + 1) * P)
                nc.tensor.matmul_mx(
                    out=dxv_t[s][:],
                    lhsT=w_codes[n][:, c_cols].bitcast(E4M3_X4),
                    lhsT_scale=w_scales[n][:, c_cols],
                    rhs=dv_codes[:, g, :].bitcast(E5M2_X4),
                    rhs_scale=dv_scales[:, g, :],
                    start=(g == 0),
                    stop=(g == PASSES - 1),
                )

        blended = {}
        back = {}
        out_rows = {}

        def blend(s):
            nxt = next_term[s % len(next_term)]
            later_tokens = dxv_t[s][:].rearrange("p (b t) -> p b t", b=B)[:, :, 1:T]
            if s % 2 == 0 or s < N_TILES - TILES_PER_BLOCK:
                nc.scalar.activation(out=nxt[:, :, 0 : T - 1], in_=later_tokens, func=ACT.Copy, scale=minus_xv[:, s : s + 1])
            else:
                nc.vector.tensor_scalar(
                    out=nxt[:, :, 0 : T - 1], in0=later_tokens, scalar1=minus_xv[:, s : s + 1], scalar2=None, op0=ALU.mult
                )
            blended[s] = work.tile([P, TOK], F32, tag="blended", name="blended%d" % s, bufs=8)
            nc.vector.scalar_tensor_tensor(
                out=blended[s][:],
                in0=dxv_t[s][:],
                scalar=xv_minus_one[:, s : s + 1],
                in1=nxt[:].rearrange("p b t -> p (b t)"),
                op0=ALU.mult,
                op1=ALU.add,
            )

        def transpose_back(s):
            if s < N_TILES - TILES_PER_BLOCK:
                back[s] = psum.tile([P, B, P], F32, tag="tr", name="back%d" % s)
            else:
                back[s] = psum.tile([P, B, P], F32, tag="dxv_t", name="back%d" % s, bufs=ACC_BANKS)
            for b in range(B):
                nc.tensor.transpose(back[s][:, b, :], blended[s][:, b * T : (b + 1) * T], ident_f32[:])

        def store(s):
            piece, i = divmod(s, STORE_TILES)
            if i == 0:
                out_rows[piece] = work.tile([P, B, STORE_TILES * P], F32, tag="out_rows", name="out_rows%d" % piece, bufs=5)
            if i == 0 or s < N_TILES - TILES_PER_BLOCK:
                nc.scalar.copy(out=out_rows[piece][:, :, i * P : (i + 1) * P], in_=back[s][:])
            else:
                nc.vector.tensor_copy(out=out_rows[piece][:, :, i * P : (i + 1) * P], in_=back[s][:])
            if s >= N_TILES - TILES_PER_BLOCK:
                nc.sync.dma_start(
                    out=out.rearrange("b t c -> t b c")[:, :, s * P : (s + 1) * P], in_=out_rows[piece][:, :, i * P : (i + 1) * P]
                )
            elif i == STORE_TILES - 1:
                c_cols = slice(piece * STORE_TILES * P, (piece + 1) * STORE_TILES * P)
                nc.sync.dma_start(out=out.rearrange("b t c -> t b c")[:, :, c_cols], in_=out_rows[piece][:])

        for r in range(N_CHUNKS + 2 + TILES_PER_BLOCK + 2):
            if 0 <= r - 2 < N_CHUNKS:
                with tc.high_priority():
                    multiply(r - 2)
            done_block, step = divmod(r - 2 - (PASSES - 1), PASSES)
            if 0 <= done_block < N_BLOCKS - 1 and step < 2:
                blend(done_block * TILES_PER_BLOCK + 2 * step)
                blend(done_block * TILES_PER_BLOCK + 2 * step + 1)
            if done_block == N_BLOCKS - 1 and step < 2:
                with tc.high_priority():
                    blend(done_block * TILES_PER_BLOCK + 2 * step)
                    blend(done_block * TILES_PER_BLOCK + 2 * step + 1)
            if 0 <= r - 6 < N_TILES:
                transpose_back(r - 6)
            if 0 <= r - 7 < N_TILES:
                store(r - 7)
            if 0 <= r - 1 < N_CHUNKS:
                quantise_w(r - 1)
            if 0 <= r < N_CHUNKS:
                regroup_w(r)
